import numpy as np
import ml_dtypes


def mxq(x, axis, fmt="e4m3"):
    dtype, down = {"e4m3": (ml_dtypes.float8_e4m3fn, 7), "e5m2": (ml_dtypes.float8_e5m2, 14)}[fmt]
    v = np.moveaxis(np.asarray(x, np.float32).astype(ml_dtypes.bfloat16).astype(np.float64), axis, -1)
    blocks = v.reshape(v.shape[:-1] + (-1, 32))
    amax = np.abs(blocks).max(-1, keepdims=True)
    byte = np.maximum(np.where(amax > 0, np.frexp(amax)[1] - 1 + 127, 0) - down, 1)
    scale = np.exp2(byte - 127.0)
    codes = (blocks / scale).astype(np.float32).astype(dtype).astype(np.float64)
    return np.moveaxis((codes * scale).reshape(v.shape), -1, axis)


WIDE = False


def mx_kscale(k):
    if not WIDE:
        return np.ones(k)
    levels = np.array([10, -10, 5, -5, 0])
    if k % 512:
        return np.exp2(np.random.permutation(np.resize(levels, k // 32))).repeat(32)
    a = np.empty((k // 512, 16))
    for p in range(k // 512):
        a[p, :8] = np.random.permutation(np.resize(levels, 8))
        for g in range(8):
            far = levels[np.abs(levels - a[p, g]) >= 10]
            a[p, g + 8] = far[np.random.randint(len(far))]
    return np.exp2(a.ravel()).repeat(32)


BF16 = ml_dtypes.bfloat16


def bf(x):
    return np.asarray(x, np.float32).astype(BF16)


def f64(x):
    return np.asarray(x).astype(np.float64)


B, C, H, W, K = 2, 1024, 32, 32, 1024
N = H * W
XS = 1.6 / C ** 0.25
CS = 0.4 / C ** 0.25


def setup_inputs():
    t = mx_kscale(K)
    u = mx_kscale(C)
    z = 1.3 * np.random.standard_normal((B, N, K)) + np.random.standard_normal((1, 1, K))
    a = np.exp(z - z.max(axis=-1, keepdims=True))
    a = a / a.sum(axis=-1, keepdims=True)
    feat = XS * (np.random.standard_normal((B, N, C)) + 0.4 * np.random.standard_normal((1, 1, C)))
    code = np.random.standard_normal((K, C)) * CS
    g = 8.0 * np.random.standard_normal((B, K, C)) * np.exp2(np.random.randint(-6, 1, (B, K, 1)))
    return {'assign': bf(a * t[None, None, :]),
            'xp': bf(feat / u[None, None, :]),
            'codebook': bf(code / u[None, :]),
            'grad_out': bf(g / t[None, :, None] * u[None, None, :])}


def reference(assign, xp, codebook, grad_out):
    assign, xp, codebook, g = f64(assign), f64(xp), f64(codebook), f64(grad_out)
    dxp = mxq(assign, 2, 'e4m3') @ mxq(g, 1, 'e5m2')
    r = np.sum(g * codebook[None], axis=2)
    dassign = (mxq(xp, 2, 'e4m3') @ mxq(g, 2, 'e5m2').transpose(0, 2, 1)) - r[:, None, :]
    return dxp, dassign

@@ -1,0 +1,326 @@
+from contextlib import ExitStack
+
+import concourse.mybir as mybir
+from concourse.masks import make_identity
+
+F32 = mybir.dt.float32
+BF16 = mybir.dt.bfloat16
+U32 = mybir.dt.uint32
+U8 = mybir.dt.uint8
+E4M3X4 = mybir.dt.float8_e4m3fn_x4
+E5M2X4 = mybir.dt.float8_e5m2_x4
+MULT = mybir.AluOpType.mult
+SUBTRACT = mybir.AluOpType.subtract
+
+IMAGES, PIXELS, CHANNELS, CODEWORDS = 2, 1024, 1024, 1024
+FLOPS = 2 * 2 * IMAGES * PIXELS * CHANNELS * CODEWORDS
+
+P = 128
+PACK = 4
+K_PASS = P * PACK
+PASSES = 2
+HALF = 512
+ROWS = 2
+UNIT = P * ROWS
+ORDER = [('A', 0, 0), ('A', 0, 1), ('A', 0, 2), ('A', 0, 3), ('X', 0, 1), ('X', 0, 0), ('X', 0, 2), ('A', 1, 0), ('A', 1, 1), ('X', 0, 3), ('A', 1, 3), ('A', 1, 2), ('X', 1, 3), ('X', 1, 2), ('X', 1, 1), ('X', 1, 0)]
+LOADS = [('gh', 0, 0, 1), ('gh', 0, 1, 1), ('gh', 0, 1, 0), ('u', ('A', 0, 0), 1), ('u', ('A', 0, 0), 0), ('gh', 0, 0, 0), ('u', ('A', 0, 2)), ('b', 1), ('u', ('X', 0, 0)), ('g', 1, 0), ('b', 0), ('g', 1, 1)]
+LATER = [(0, ('u', ('X', 0, 2))), (0, ('u', ('A', 1, 0))), (1, ('u', ('X', 1, 2))), (4, ('u', ('A', 1, 2))), (6, ('u', ('X', 1, 0)))]
+HEAD = [('gk', 0, 0, 1), ('fg', 0, 1, 1), ('qk', 0, 0, 1), ('fg', 0, 1, 0), ('gk', 0, 1, 0), ('gk', 0, 1, 1), ('fg', 0, 0, 1), ('flip', 1), ('flip', 0), ('qk', 0, 1, 1), ('fg', 0, 0, 0), ('qk', 0, 1, 0), ('gk', 0, 0, 0), ('qk', 0, 0, 0), ('qu', 0)]
+PLACE = {(1, 2): [('r', 0, 1, 0)], (2, 2): [('gk', 1, 0, 1)], (3, 2): [('gk', 1, 1, 1), ('qc', 0, 0, 0), ('r', 0, 1, 3)], (4, 0): [('fg', 1, 1, 1)], (4, 6): [('qk', 1, 1, 0)], (8, 6): [('r', 1, 0, 0)], (12, 0): [('sp', 1, 1)], (8, 5): [('r', 1, 0, 2)], (1, 3): [('r', 0, 1, 1), ('qc', 0, 1, 0)], (6, 1): [('qk', 1, 0, 0)], (10, 5): [('qc', 1, 1, 0), ('r', 1, 1, 0)], (2, 1): [('fg', 1, 0, 1)], (11, 5): [('qc', 1, 0, 0)], (1, 1): [('qc', 0, 1, 1)], (7, 1): [('fg', 1, 1, 0)], (8, 1): [('r', 1, 0, 1)], (11, 0): [('r', 1, 1, 2)], (4, 2): [('sp', 0, 1), ('sp', 0, 0)], (11, 6): [('sp', 1, 0)], (1, 0): [('qc', 0, 0, 1)], (9, 6): [('fg', 1, 0, 0)], (2, 6): [('r', 0, 0, 0)], (1, 5): [('r', 0, 1, 2)], (2, 5): [('r', 0, 0, 2)], (3, 0): [('r', 0, 0, 3)], (8, 3): [('r', 1, 1, 3)], (9, 3): [('r', 1, 0, 3), ('r', 1, 1, 1)], (4, 4): [('gk', 1, 1, 0)], (3, 1): [('qk', 1, 0, 1), ('r', 0, 0, 1)], (5, 5): [('gk', 1, 0, 0)], (6, 5): [('qk', 1, 1, 1)], (12, 1): [('qc', 1, 0, 1), ('qc', 1, 1, 1)]}
+FILL_ENGINE = {('gk', 0, 0, 1): 'V', ('gk', 1, 0, 0): 'S', ('gk', 1, 1, 0): 'S', ('gk', 1, 0, 1): 'V', ('sp', 0, 0): 'S', ('gk', 0, 1, 0): 'V', ('sp', 1, 0): 'S', ('sp', 1, 1): 'S', ('sp', 0, 1): 'S', ('gk', 0, 0, 0): 'V', ('gk', 1, 1, 1): 'S', ('gk', 0, 1, 1): 'V'}
+FLIP_ENGINES = {('A', 1, 0): 'VS'}
+COPY_ENGINE = {(('A', 0, 3), 0): 'V', (('A', 0, 3), 1): 'V', (('A', 0, 3), 3): 'V', (('A', 0, 3), 2): 'V'}
+SORTED = {('fg', 1, 1, 0): 'S', ('X', 1, 1): 'V', ('fg', 1, 0, 0): 'S', ('X', 1, 0): 'V'}
+PAIR = True
+FINE = 4
+HALF_FIRST = 2
+UNIT_BUFS = 4
+ROW_BUFS = 5
+RESULT_BUFS = 4
+FLIP_BANKS = 4
+SUM_BANKS = 4
+
+
+def tile_lvc_pb_v_kernel(tc, assign, xp, codebook, grad_out, out_0, out_1):
+    nc = tc.nc
+    with ExitStack() as ctx:
+        keep = ctx.enter_context(tc.tile_pool(name="keep", bufs=1))
+        stream = ctx.enter_context(tc.tile_pool(name="stream", bufs=3))
+        flips = ctx.enter_context(tc.psum_pool(name="flips", bufs=FLIP_BANKS))
+        sums = ctx.enter_context(tc.psum_pool(name="sums", bufs=SUM_BANKS))
+
+        ident = keep.tile([P, P], F32, name="ident")
+        make_identity(nc, ident[:])
+
+        grad = {}
+        grad_k_codes, grad_k_scales = {}, {}
+        grad_c_codes, grad_c_scales = {}, {}
+        r_column, r_rows = {}, {}
+        for b in range(IMAGES):
+            for g in range(PASSES):
+                grad[b, g] = keep.tile([P, PACK, CHANNELS], BF16, name="grad_%d_%d" % (b, g), align_bytes=64)
+            grad_k_codes[b] = keep.tile([P, PASSES, CHANNELS], U32, name="grad_k_codes_%d" % b, align_bytes=64)
+            grad_k_scales[b] = keep.tile([P, PASSES, CHANNELS], U8, name="grad_k_scales_%d" % b, align_bytes=64)
+            grad_c_codes[b] = keep.tile([P, PASSES, CODEWORDS], U32, name="grad_c_codes_%d" % b, align_bytes=64)
+            grad_c_scales[b] = keep.tile([P, PASSES, CODEWORDS], U8, name="grad_c_scales_%d" % b, align_bytes=64)
+            r_column[b] = keep.tile([P, PASSES * PACK], F32, name="r_column_%d" % b)
+            r_rows[b] = keep.tile([P, CODEWORDS], F32, name="r_rows_%d" % b)
+        words = {}
+        for g in range(PASSES):
+            words[g] = keep.tile([P, PACK, CHANNELS], BF16, name="book_%d" % g, align_bytes=64)
+        book = words
+
+        def codeword_rows(matrix, g):
+            return matrix[g * K_PASS : (g + 1) * K_PASS, :].rearrange("(p j) c -> p j c", j=PACK)
+
+        def load_grad_half(b, g, half):
+            cols = slice(half * HALF, (half + 1) * HALF)
+            nc.sync.dma_start(out=grad[b, g][:, :, cols], in_=codeword_rows(grad_out[b], g)[:, :, cols])
+
+        def load_grad(b, g):
+            nc.sync.dma_start(out=grad[b, g][:], in_=codeword_rows(grad_out[b], g))
+
+        def load_book(g):
+            nc.sync.dma_start(out=book[g][:], in_=codeword_rows(codebook, g))
+
+        raw = {}
+
+        def load_rows(u, part=None):
+            kind, b, i = u
+            source = (assign if kind == "A" else xp)[b, (i // 2) * 2 * UNIT : (i // 2 + 1) * 2 * UNIT, :].rearrange(
+                "(p j) k -> p j k", j=2 * ROWS
+            )
+            key = (kind, b, i // 2)
+            if key not in raw:
+                rows = stream.tile([P, 2 * ROWS, 1024], BF16, name="rows", bufs=ROW_BUFS, align_bytes=64)
+                raw[key] = rows
+            span = slice(0, 2 * ROWS) if part is None else slice(part * ROWS, (part + 1) * ROWS)
+            nc.sync.dma_start(out=raw[key][:, span, :], in_=source[:, span, :])
+
+        def sort_words(words, engine):
+            ordered = stream.tile([P, 2, 2, 2, P], F32, name="ordered", bufs=2)
+            copy = nc.scalar.copy if engine == "S" else nc.vector.tensor_copy
+            return ordered, copy
+
+        grouped = {}
+
+        def flip_unit(u):
+            engines = FLIP_ENGINES.get(u, "SS")
+            kind, b, i = u
+            wide = raw[kind, b, i // 2][:].bitcast(F32)[:, (i % 2) * ROWS : (i % 2 + 1) * ROWS, :]
+            engine = SORTED.get(u)
+            if engine:
+                ordered, copy = sort_words(None, engine)
+                copy(out=ordered[:].rearrange("p j h w n -> p (j h) w n"), in_=wide.rearrange("p j (h n w) -> p (j h) w n", h=PASSES, w=2))
+            stage = stream.tile([P, ROWS, PASSES, P, PACK], BF16, name="unit_grouped", bufs=UNIT_BUFS, align_bytes=64)
+            for j in range(ROWS):
+                bank = flips.tile([P, PASSES, 2, P], F32, name="flip_bank")
+                for h in range(PASSES):
+                    for w in range(2):
+                        columns = ordered[:, j, h, w, :] if engine else wide[:, j, 256 * h + w : 256 * (h + 1) : 2]
+                        nc.tensor.transpose(bank[:, h, w, :], columns, ident[:])
+                copy = nc.scalar.copy if engines[j] == "S" else nc.vector.tensor_copy
+                copy(out=stage[:, j].bitcast(F32), in_=bank[:].rearrange("p h w n -> p h n w"))
+            grouped[u] = stage
+
+        coded = {}
+
+        def quantize_unit(u):
+            stage = grouped.pop(u)
+            codes = stream.tile([P, ROWS * PASSES * P], U32, name="unit_codes", align_bytes=64)
+            scales = stream.tile([P, ROWS * PASSES * P], U8, name="unit_scales", align_bytes=64)
+            nc.vector.quantize_mx(
+                out=codes[:].bitcast(E4M3X4), scales=scales[:], in_=stage[:].rearrange("p j h n t -> p (j h n t)")
+            )
+            coded[u] = (codes, scales)
+
+        result = {}
+
+        def multiply(u, j, half):
+            kind, b, i = u
+            codes, scales = coded[u]
+            moving, moving_scales = (
+                (grad_k_codes[b], grad_k_scales[b]) if kind == "A" else (grad_c_codes[b], grad_c_scales[b])
+            )
+            acc = sums.tile([P, HALF], F32, name="acc")
+            cols = slice(half * HALF, (half + 1) * HALF)
+            for h in range(PASSES):
+                own = slice((j * PASSES + h) * P, (j * PASSES + h + 1) * P)
+                nc.tensor.matmul_mx(
+                    out=acc[:],
+                    lhsT=codes[:, own].bitcast(E4M3X4),
+                    lhsT_scale=scales[:, own],
+                    rhs=moving[:, h, cols].bitcast(E5M2X4),
+                    rhs_scale=moving_scales[:, h, cols],
+                    start=(h == 0),
+                    stop=(h == PASSES - 1),
+                )
+            if u not in result:
+                result[u] = stream.tile([P, ROWS, 1024], F32, name="result", bufs=RESULT_BUFS)
+            return acc
+
+        def finish(u, j, half, acc, engine="S"):
+            kind, b, i = u
+            cols = slice(half * HALF, (half + 1) * HALF)
+            target = result[u][:, j, cols]
+            if kind == "A":
+                copy = nc.scalar.copy if engine == "S" else nc.vector.tensor_copy
+                copy(out=target, in_=acc[:])
+            else:
+                nc.vector.tensor_tensor(
+                    out=target.rearrange("p (q j) -> p q j", j=PACK),
+                    in0=acc[:].rearrange("p (j q) -> p q j", j=PACK),
+                    in1=r_rows[b][:, cols].rearrange("p (q j) -> p q j", j=PACK),
+                    op=SUBTRACT,
+                )
+
+        def store(u, rows=slice(0, ROWS), cols=slice(0, 1024)):
+            kind, b, i = u
+            target = (out_0 if kind == "A" else out_1)[b, (i // 2) * 2 * UNIT : (i // 2 + 1) * 2 * UNIT, :].rearrange(
+                "(p j) c -> p j c", j=2 * ROWS
+            )[:, (i % 2) * ROWS : (i % 2 + 1) * ROWS, :]
+            nc.sync.dma_start(out=target[:, rows, cols], in_=result[u][:, rows, cols])
+
+        grad_stage = {}
+
+        def group_grad_k(b, g, half, engine):
+            cols = slice(half * HALF, (half + 1) * HALF)
+            stage = stream.tile([P, HALF, PACK], BF16, name="grad_k_grouped", align_bytes=64)
+            copy = nc.scalar.copy if engine == "S" else nc.vector.tensor_copy
+            copy(
+                out=stage[:].rearrange("p (c i) t -> p c t i", i=4),
+                in_=grad[b, g][:, :, cols].rearrange("p t (c i) -> p c t i", i=4),
+            )
+            grad_stage["k", b, g, half] = stage
+
+        def quantize_grad_k(b, g, half):
+            cols = slice(half * HALF, (half + 1) * HALF)
+            nc.vector.quantize_mx(
+                out=grad_k_codes[b][:, g, cols].bitcast(E5M2X4),
+                scales=grad_k_scales[b][:, g, cols],
+                in_=grad_stage.pop(("k", b, g, half))[:].rearrange("p c t -> p (c t)"),
+            )
+
+        def flip_grad(b, g, h):
+            engines = FLIP_ENGINES.get(("fg", b, g, h), "SS")
+            wide = grad[b, g][:].bitcast(F32)
+            engine = SORTED.get(("fg", b, g, h))
+            if engine:
+                ordered, copy = sort_words(None, engine)
+                copy(out=ordered[:].rearrange("p j h w n -> p (j h) w n"), in_=wide[:, :, 256 * h : 256 * (h + 1)].rearrange("p j (n w) -> p j w n", w=2))
+            stage = stream.tile([P, PACK, P, PACK], BF16, name="grad_c_grouped", bufs=4, align_bytes=64)
+            for pair in range(2):
+                bank = flips.tile([P, 2, 2, P], F32, name="flip_bank")
+                for jj in range(2):
+                    for w in range(2):
+                        columns = ordered[:, pair, jj, w, :] if engine else wide[:, 2 * pair + jj, 256 * h + w : 256 * (h + 1) : 2]
+                        nc.tensor.transpose(bank[:, jj, w, :], columns, ident[:])
+                copy = nc.scalar.copy if engines[pair] == "S" else nc.vector.tensor_copy
+                copy(
+                    out=stage[:, 2 * pair : 2 * pair + 2].bitcast(F32), in_=bank[:].rearrange("p j w n -> p j n w")
+                )
+            grad_stage["c", b, g, h] = stage
+
+        def quantize_grad_c(b, g, h):
+            cols = slice(g * K_PASS, (g + 1) * K_PASS)
+            nc.vector.quantize_mx(
+                out=grad_c_codes[b][:, h, cols].bitcast(E5M2X4),
+                scales=grad_c_scales[b][:, h, cols],
+                in_=grad_stage.pop(("c", b, g, h))[:].rearrange("p j n t -> p (j n t)"),
+            )
+
+        def sum_r(b, g, j):
+            product = stream.tile([P, CHANNELS], F32, name="product", bufs=1)
+            nc.vector.scalar_tensor_tensor(
+                out=product[:],
+                in0=grad[b, g][:, j, :],
+                scalar=1.0,
+                in1=book[g][:, j, :],
+                op0=MULT,
+                op1=MULT,
+                accum_out=r_column[b][:, g * PACK + j : g * PACK + j + 1],
+            )
+
+        def spread_r(b, g, engine):
+            bank = flips.tile([P, PACK, P], F32, name="flip_bank")
+            for j in range(PACK):
+                m = g * PACK + j
+                nc.tensor.transpose(bank[:, j, :], r_column[b][:, m : m + 1].to_broadcast([P, P]), ident[:])
+            copy = nc.scalar.copy if engine == "S" else nc.vector.tensor_copy
+            copy(
+                out=r_rows[b][:, g * K_PASS : (g + 1) * K_PASS].rearrange("p (q j) -> p q j", j=PACK),
+                in_=bank[:].rearrange("p j q -> p q j"),
+            )
+
+        def fill(f):
+            kind, b, g, *rest = f
+            engine = FILL_ENGINE.get(f, "S" if kind == "sp" else "V")
+            if kind == "gk":
+                group_grad_k(b, g, rest[0], engine)
+            elif kind == "qk":
+                quantize_grad_k(b, g, rest[0])
+            elif kind == "fg":
+                flip_grad(b, g, rest[0])
+            elif kind == "qc":
+                quantize_grad_c(b, g, rest[0])
+            elif kind == "r":
+                sum_r(b, g, rest[0])
+            else:
+                spread_r(b, g, engine)
+
+        def load(x):
+            if x[0] == "gh":
+                load_grad_half(*x[1:])
+            elif x[0] == "g":
+                load_grad(*x[1:])
+            elif x[0] == "b":
+                load_book(x[1])
+            else:
+                load_rows(*x[1:])
+
+        with tc.manual_schedule():
+            done = set()
+            for x in LOADS:
+                load(x)
+            for f in HEAD:
+                if f[0] == "flip":
+                    flip_unit(ORDER[f[1]])
+                    done.add(f[1])
+                elif f[0] == "qu":
+                    quantize_unit(ORDER[f[1]])
+                    done.add(("q", f[1]))
+                else:
+                    fill(f)
+            later = list(LATER)
+            n = len(ORDER)
+            for s, u in enumerate(ORDER):
+                for f in PLACE.get((s, 0), []):
+                    fill(f)
+                ahead = ([s + 2, s + 3] if s % 2 == 0 else []) if PAIR else [s + 2]
+                for d in ahead:
+                    if d < n and d not in done:
+                        done.add(d)
+                        flip_unit(ORDER[d])
+                for f in PLACE.get((s, 1), []):
+                    fill(f)
+                if s + 1 < n and ("q", s + 1) not in done:
+                    quantize_unit(ORDER[s + 1])
+                for f in PLACE.get((s, 2), []):
+                    fill(f)
+                last = s == n - 1
+                if s < HALF_FIRST:
+                    groups = [(half, j) for half in range(2) for j in range(ROWS)]
+                else:
+                    groups = [(half, j) for j in range(ROWS) for half in range(2)]
+                for k, (half, j) in enumerate(groups):
+                    finish(u, j, half, multiply(u, j, half), COPY_ENGINE.get((u, k), "S"))
+                    for f in PLACE.get((s, 3 + k), []):
+                        fill(f)
+                    if last:
+                        store(u, slice(j, j + 1), slice(half * HALF, (half + 1) * HALF))
+                    elif s >= n - FINE and half == 1:
+                        store(u, slice(j, j + 1))
+                while later and later[0][0] <= s:
+                    load(later.pop(0)[1])
+                if s < n - FINE:
+                    store(u)

@@ -22,19 +22,19 @@ PASSES = 2
 HALF = 512
 ROWS = 2
 UNIT = P * ROWS
-ORDER = [('A', 0, 0), ('A', 0, 1), ('A', 0, 2), ('A', 0, 3), ('X', 0, 1), ('X', 0, 0), ('X', 0, 2), ('A', 1, 0), ('A', 1, 1), ('X', 0, 3), ('A', 1, 3), ('A', 1, 2), ('X', 1, 3), ('X', 1, 2), ('X', 1, 1), ('X', 1, 0)]
-LOADS = [('gh', 0, 0, 1), ('gh', 0, 1, 1), ('gh', 0, 1, 0), ('u', ('A', 0, 0), 1), ('u', ('A', 0, 0), 0), ('gh', 0, 0, 0), ('u', ('A', 0, 2)), ('b', 1), ('u', ('X', 0, 0)), ('g', 1, 0), ('b', 0), ('g', 1, 1)]
-LATER = [(0, ('u', ('X', 0, 2))), (0, ('u', ('A', 1, 0))), (1, ('u', ('X', 1, 2))), (4, ('u', ('A', 1, 2))), (6, ('u', ('X', 1, 0)))]
-HEAD = [('gk', 0, 0, 1), ('fg', 0, 1, 1), ('qk', 0, 0, 1), ('fg', 0, 1, 0), ('gk', 0, 1, 0), ('gk', 0, 1, 1), ('fg', 0, 0, 1), ('flip', 1), ('flip', 0), ('qk', 0, 1, 1), ('fg', 0, 0, 0), ('qk', 0, 1, 0), ('gk', 0, 0, 0), ('qk', 0, 0, 0), ('qu', 0)]
-PLACE = {(1, 2): [('r', 0, 1, 0)], (2, 2): [('gk', 1, 0, 1)], (3, 2): [('gk', 1, 1, 1), ('qc', 0, 0, 0), ('r', 0, 1, 3)], (4, 0): [('fg', 1, 1, 1)], (4, 6): [('qk', 1, 1, 0)], (8, 6): [('r', 1, 0, 0)], (12, 0): [('sp', 1, 1)], (8, 5): [('r', 1, 0, 2)], (1, 3): [('r', 0, 1, 1), ('qc', 0, 1, 0)], (6, 1): [('qk', 1, 0, 0)], (10, 5): [('qc', 1, 1, 0), ('r', 1, 1, 0)], (2, 1): [('fg', 1, 0, 1)], (11, 5): [('qc', 1, 0, 0)], (1, 1): [('qc', 0, 1, 1)], (7, 1): [('fg', 1, 1, 0)], (8, 1): [('r', 1, 0, 1)], (11, 0): [('r', 1, 1, 2)], (4, 2): [('sp', 0, 1), ('sp', 0, 0)], (11, 6): [('sp', 1, 0)], (1, 0): [('qc', 0, 0, 1)], (9, 6): [('fg', 1, 0, 0)], (2, 6): [('r', 0, 0, 0)], (1, 5): [('r', 0, 1, 2)], (2, 5): [('r', 0, 0, 2)], (3, 0): [('r', 0, 0, 3)], (8, 3): [('r', 1, 1, 3)], (9, 3): [('r', 1, 0, 3), ('r', 1, 1, 1)], (4, 4): [('gk', 1, 1, 0)], (3, 1): [('qk', 1, 0, 1), ('r', 0, 0, 1)], (5, 5): [('gk', 1, 0, 0)], (6, 5): [('qk', 1, 1, 1)], (12, 1): [('qc', 1, 0, 1), ('qc', 1, 1, 1)]}
-FILL_ENGINE = {('gk', 0, 0, 1): 'V', ('gk', 1, 0, 0): 'S', ('gk', 1, 1, 0): 'S', ('gk', 1, 0, 1): 'V', ('sp', 0, 0): 'S', ('gk', 0, 1, 0): 'V', ('sp', 1, 0): 'S', ('sp', 1, 1): 'S', ('sp', 0, 1): 'S', ('gk', 0, 0, 0): 'V', ('gk', 1, 1, 1): 'S', ('gk', 0, 1, 1): 'V'}
-FLIP_ENGINES = {('A', 1, 0): 'VS'}
-COPY_ENGINE = {(('A', 0, 3), 0): 'V', (('A', 0, 3), 1): 'V', (('A', 0, 3), 3): 'V', (('A', 0, 3), 2): 'V'}
-SORTED = {('fg', 1, 1, 0): 'S', ('X', 1, 1): 'V', ('fg', 1, 0, 0): 'S', ('X', 1, 0): 'V'}
-PAIR = True
+ORDER = [('A', 0, 0), ('A', 0, 1), ('A', 0, 3), ('A', 0, 2), ('X', 0, 1), ('X', 0, 0), ('X', 0, 3), ('A', 1, 1), ('X', 0, 2), ('A', 1, 0), ('A', 1, 2), ('A', 1, 3), ('X', 1, 0), ('X', 1, 2), ('X', 1, 1), ('X', 1, 3)]
+LOADS = [('gh', 0, 0, 0), ('gh', 0, 1, 0), ('gh', 0, 1, 1), ('u', ('A', 0, 0), 1), ('gh', 0, 0, 1), ('u', ('A', 0, 0), 0), ('u', ('A', 0, 2)), ('g', 1, 0), ('b', 1), ('g', 1, 1), ('b', 0)]
+LATER = [(0, ('u', ('X', 0, 0))), (0, ('u', ('X', 0, 2))), (0, ('u', ('A', 1, 2))), (0, ('u', ('X', 1, 0))), (1, ('u', ('A', 1, 0))), (6, ('u', ('X', 1, 2)))]
+HEAD = [('gk', 0, 0, 0), ('fg', 0, 0, 0), ('fg', 0, 1, 0), ('gk', 0, 1, 0), ('qk', 0, 0, 0), ('qc', 0, 0, 0), ('qk', 0, 1, 0), ('qc', 0, 1, 0), ('fg', 0, 1, 1), ('gk', 0, 0, 1), ('flip', 1), ('flip', 0), ('qu', 0), ('gk', 0, 1, 1), ('fg', 0, 0, 1)]
+PLACE = {(0, 2): [('gk', 1, 0, 0), ('qk', 0, 1, 1), ('gk', 1, 0, 1)], (1, 2): [('qc', 0, 1, 1)], (2, 2): [('qk', 1, 1, 0)], (3, 2): [('r', 0, 0, 0)], (12, 0): [('r', 1, 1, 1), ('sp', 1, 1)], (1, 3): [('r', 1, 0, 1), ('fg', 1, 1, 1)], (10, 0): [('r', 1, 0, 3)], (2, 0): [('r', 0, 0, 1)], (8, 1): [('r', 1, 0, 2)], (2, 5): [('r', 1, 1, 0)], (11, 5): [('r', 1, 1, 2)], (4, 2): [('sp', 0, 0)], (1, 0): [('qc', 0, 0, 1)], (10, 5): [('r', 1, 1, 3)], (3, 4): [('qc', 1, 1, 1)], (6, 0): [('qk', 1, 0, 1)], (6, 2): [('qk', 1, 1, 1)], (0, 4): [('fg', 1, 0, 0)], (11, 1): [('qc', 1, 0, 1), ('sp', 1, 0)], (0, 6): [('r', 0, 1, 1), ('r', 0, 1, 2)], (1, 4): [('qk', 1, 0, 0)], (8, 2): [('qc', 1, 0, 0)], (3, 1): [('sp', 0, 1)], (1, 1): [('r', 0, 1, 3), ('gk', 1, 1, 0)], (1, 5): [('fg', 1, 1, 0), ('r', 0, 0, 3), ('r', 0, 1, 0)], (3, 5): [('r', 0, 0, 2), ('fg', 1, 0, 1)], (5, 5): [('gk', 1, 1, 1)], (3, 6): [('qc', 1, 1, 0)], (9, 1): [('r', 1, 0, 0)], (0, 1): [('qk', 0, 0, 1)]}
+FILL_ENGINE = {('gk', 0, 0, 1): 'V', ('gk', 1, 0, 0): 'S', ('gk', 1, 1, 0): 'S', ('gk', 1, 0, 1): 'V', ('sp', 1, 0): 'S', ('sp', 1, 1): 'S', ('sp', 0, 1): 'S', ('gk', 0, 0, 0): 'S', ('gk', 1, 1, 1): 'S', ('sp', 0, 0): 'S', ('gk', 0, 1, 0): 'V', ('gk', 0, 1, 1): 'S'}
+FLIP_ENGINES = {('A', 0, 2): 'SV', ('X', 0, 3): 'VS', ('A', 0, 0): 'VV', ('fg', 1, 0, 0): 'VS'}
+COPY_ENGINE = {(('A', 0, 0), 0): 'V'}
+SORTED = {('X', 1, 3): 'S', ('X', 1, 1): 'V', ('A', 1, 0): 'S', ('A', 1, 3): 'S', ('A', 1, 1): 'S', ('X', 1, 2): 'V', ('A', 1, 2): 'V'}
+PAIR = False
 FINE = 4
 HALF_FIRST = 2
-UNIT_BUFS = 4
+UNIT_BUFS = 3
 ROW_BUFS = 5
 RESULT_BUFS = 4
 FLIP_BANKS = 4
@@ -58,7 +58,8 @@ def tile_lvc_pb_v_kernel(tc, assign, xp, codebook, grad_out, out_0, out_1):
         r_column, r_rows = {}, {}
         for b in range(IMAGES):
             for g in range(PASSES):
-                grad[b, g] = keep.tile([P, PACK, CHANNELS], BF16, name="grad_%d_%d" % (b, g), align_bytes=64)
+                shape = [P, 2, PACK, HALF] if b == 0 else [P, PACK, CHANNELS]
+                grad[b, g] = keep.tile(shape, BF16, name="grad_%d_%d" % (b, g), align_bytes=64)
             grad_k_codes[b] = keep.tile([P, PASSES, CHANNELS], U32, name="grad_k_codes_%d" % b, align_bytes=64)
             grad_k_scales[b] = keep.tile([P, PASSES, CHANNELS], U8, name="grad_k_scales_%d" % b, align_bytes=64)
             grad_c_codes[b] = keep.tile([P, PASSES, CODEWORDS], U32, name="grad_c_codes_%d" % b, align_bytes=64)
@@ -75,7 +76,12 @@ def tile_lvc_pb_v_kernel(tc, assign, xp, codebook, grad_out, out_0, out_1):
 
         def load_grad_half(b, g, half):
             cols = slice(half * HALF, (half + 1) * HALF)
-            nc.sync.dma_start(out=grad[b, g][:, :, cols], in_=codeword_rows(grad_out[b], g)[:, :, cols])
+            nc.sync.dma_start(out=grad[b, g][:, half], in_=codeword_rows(grad_out[b], g)[:, :, cols])
+
+        def grad_half(b, g, half):
+            if b == 0:
+                return grad[b, g][:, half]
+            return grad[b, g][:, :, half * HALF : (half + 1) * HALF]
 
         def load_grad(b, g):
             nc.sync.dma_start(out=grad[b, g][:], in_=codeword_rows(grad_out[b], g))
@@ -184,12 +190,11 @@ def tile_lvc_pb_v_kernel(tc, assign, xp, codebook, grad_out, out_0, out_1):
         grad_stage = {}
 
         def group_grad_k(b, g, half, engine):
-            cols = slice(half * HALF, (half + 1) * HALF)
             stage = stream.tile([P, HALF, PACK], BF16, name="grad_k_grouped", align_bytes=64)
             copy = nc.scalar.copy if engine == "S" else nc.vector.tensor_copy
             copy(
                 out=stage[:].rearrange("p (c i) t -> p c t i", i=4),
-                in_=grad[b, g][:, :, cols].rearrange("p t (c i) -> p c t i", i=4),
+                in_=grad_half(b, g, half).rearrange("p t (c i) -> p c t i", i=4),
             )
             grad_stage["k", b, g, half] = stage
 
@@ -203,17 +208,17 @@ def tile_lvc_pb_v_kernel(tc, assign, xp, codebook, grad_out, out_0, out_1):
 
         def flip_grad(b, g, h):
             engines = FLIP_ENGINES.get(("fg", b, g, h), "SS")
-            wide = grad[b, g][:].bitcast(F32)
+            wide = grad_half(b, g, h).bitcast(F32)
             engine = SORTED.get(("fg", b, g, h))
             if engine:
                 ordered, copy = sort_words(None, engine)
-                copy(out=ordered[:].rearrange("p j h w n -> p (j h) w n"), in_=wide[:, :, 256 * h : 256 * (h + 1)].rearrange("p j (n w) -> p j w n", w=2))
+                copy(out=ordered[:].rearrange("p j h w n -> p (j h) w n"), in_=wide.rearrange("p j (n w) -> p j w n", w=2))
             stage = stream.tile([P, PACK, P, PACK], BF16, name="grad_c_grouped", bufs=4, align_bytes=64)
             for pair in range(2):
                 bank = flips.tile([P, 2, 2, P], F32, name="flip_bank")
                 for jj in range(2):
                     for w in range(2):
-                        columns = ordered[:, pair, jj, w, :] if engine else wide[:, 2 * pair + jj, 256 * h + w : 256 * (h + 1) : 2]
+                        columns = ordered[:, pair, jj, w, :] if engine else wide[:, 2 * pair + jj, w::2]
                         nc.tensor.transpose(bank[:, jj, w, :], columns, ident[:])
                 copy = nc.scalar.copy if engines[pair] == "S" else nc.vector.tensor_copy
                 copy(
@@ -230,12 +235,13 @@ def tile_lvc_pb_v_kernel(tc, assign, xp, codebook, grad_out, out_0, out_1):
             )
 
         def sum_r(b, g, j):
-            product = stream.tile([P, CHANNELS], F32, name="product", bufs=1)
+            product = stream.tile([P, 2, HALF], F32, name="product", bufs=1)
+            row = grad[b, g][:, :, j, :] if b == 0 else grad[b, g][:, j, :].rearrange("p (h c) -> p h c", h=2)
             nc.vector.scalar_tensor_tensor(
                 out=product[:],
-                in0=grad[b, g][:, j, :],
+                in0=row,
                 scalar=1.0,
-                in1=book[g][:, j, :],
+                in1=book[g][:, j, :].rearrange("p (h c) -> p h c", h=2),
                 op0=MULT,
                 op1=MULT,
                 accum_out=r_column[b][:, g * PACK + j : g * PACK + j + 1],

@@ -22,15 +22,15 @@ PASSES = 2
 HALF = 512
 ROWS = 2
 UNIT = P * ROWS
-ORDER = [('A', 0, 0), ('A', 0, 1), ('A', 0, 3), ('A', 0, 2), ('X', 0, 1), ('X', 0, 0), ('X', 0, 3), ('A', 1, 1), ('X', 0, 2), ('A', 1, 0), ('A', 1, 2), ('A', 1, 3), ('X', 1, 0), ('X', 1, 2), ('X', 1, 1), ('X', 1, 3)]
-LOADS = [('gh', 0, 0, 0), ('gh', 0, 1, 0), ('gh', 0, 1, 1), ('u', ('A', 0, 0), 1), ('gh', 0, 0, 1), ('u', ('A', 0, 0), 0), ('u', ('A', 0, 2)), ('g', 1, 0), ('b', 1), ('g', 1, 1), ('b', 0)]
-LATER = [(0, ('u', ('X', 0, 0))), (0, ('u', ('X', 0, 2))), (0, ('u', ('A', 1, 2))), (0, ('u', ('X', 1, 0))), (1, ('u', ('A', 1, 0))), (6, ('u', ('X', 1, 2)))]
-HEAD = [('gk', 0, 0, 0), ('fg', 0, 0, 0), ('fg', 0, 1, 0), ('gk', 0, 1, 0), ('qk', 0, 0, 0), ('qc', 0, 0, 0), ('qk', 0, 1, 0), ('qc', 0, 1, 0), ('fg', 0, 1, 1), ('gk', 0, 0, 1), ('flip', 1), ('flip', 0), ('qu', 0), ('gk', 0, 1, 1), ('fg', 0, 0, 1)]
-PLACE = {(0, 2): [('gk', 1, 0, 0), ('qk', 0, 1, 1), ('gk', 1, 0, 1)], (1, 2): [('qc', 0, 1, 1)], (2, 2): [('qk', 1, 1, 0)], (3, 2): [('r', 0, 0, 0)], (12, 0): [('r', 1, 1, 1), ('sp', 1, 1)], (1, 3): [('r', 1, 0, 1), ('fg', 1, 1, 1)], (10, 0): [('r', 1, 0, 3)], (2, 0): [('r', 0, 0, 1)], (8, 1): [('r', 1, 0, 2)], (2, 5): [('r', 1, 1, 0)], (11, 5): [('r', 1, 1, 2)], (4, 2): [('sp', 0, 0)], (1, 0): [('qc', 0, 0, 1)], (10, 5): [('r', 1, 1, 3)], (3, 4): [('qc', 1, 1, 1)], (6, 0): [('qk', 1, 0, 1)], (6, 2): [('qk', 1, 1, 1)], (0, 4): [('fg', 1, 0, 0)], (11, 1): [('qc', 1, 0, 1), ('sp', 1, 0)], (0, 6): [('r', 0, 1, 1), ('r', 0, 1, 2)], (1, 4): [('qk', 1, 0, 0)], (8, 2): [('qc', 1, 0, 0)], (3, 1): [('sp', 0, 1)], (1, 1): [('r', 0, 1, 3), ('gk', 1, 1, 0)], (1, 5): [('fg', 1, 1, 0), ('r', 0, 0, 3), ('r', 0, 1, 0)], (3, 5): [('r', 0, 0, 2), ('fg', 1, 0, 1)], (5, 5): [('gk', 1, 1, 1)], (3, 6): [('qc', 1, 1, 0)], (9, 1): [('r', 1, 0, 0)], (0, 1): [('qk', 0, 0, 1)]}
-FILL_ENGINE = {('gk', 0, 0, 1): 'V', ('gk', 1, 0, 0): 'S', ('gk', 1, 1, 0): 'S', ('gk', 1, 0, 1): 'V', ('sp', 1, 0): 'S', ('sp', 1, 1): 'S', ('sp', 0, 1): 'S', ('gk', 0, 0, 0): 'S', ('gk', 1, 1, 1): 'S', ('sp', 0, 0): 'S', ('gk', 0, 1, 0): 'V', ('gk', 0, 1, 1): 'S'}
-FLIP_ENGINES = {('A', 0, 2): 'SV', ('X', 0, 3): 'VS', ('A', 0, 0): 'VV', ('fg', 1, 0, 0): 'VS'}
-COPY_ENGINE = {(('A', 0, 0), 0): 'V'}
-SORTED = {('X', 1, 3): 'S', ('X', 1, 1): 'V', ('A', 1, 0): 'S', ('A', 1, 3): 'S', ('A', 1, 1): 'S', ('X', 1, 2): 'V', ('A', 1, 2): 'V'}
+ORDER = [('A', 0, 0), ('A', 0, 1), ('A', 0, 2), ('A', 0, 3), ('X', 0, 0), ('X', 0, 3), ('X', 0, 1), ('A', 1, 3), ('X', 0, 2), ('A', 1, 1), ('A', 1, 2), ('A', 1, 0), ('X', 1, 1), ('X', 1, 0), ('X', 1, 2), ('X', 1, 3)]
+LOADS = [('gh', 0, 0, 0), ('gh', 0, 1, 1), ('gh', 0, 1, 0), ('u', ('A', 0, 0), 0), ('gh', 0, 0, 1), ('u', ('A', 0, 0), 1), ('u', ('A', 0, 2)), ('b', 1), ('g', 1, 1), ('g', 1, 0), ('b', 0)]
+LATER = [(0, ('u', ('X', 0, 0))), (0, ('u', ('X', 0, 2))), (0, ('u', ('A', 1, 2))), (0, ('u', ('X', 1, 0))), (3, ('u', ('A', 1, 0))), (6, ('u', ('X', 1, 2)))]
+HEAD = [('gk', 0, 0, 0), ('fg', 0, 0, 0), ('gk', 0, 1, 1), ('fg', 0, 1, 0), ('qk', 0, 0, 0), ('fg', 0, 1, 1), ('flip', 0), ('gk', 0, 1, 0), ('qk', 0, 1, 1), ('flip', 1), ('qc', 0, 0, 0), ('gk', 0, 0, 1), ('qk', 0, 1, 0), ('fg', 0, 0, 1), ('qc', 0, 1, 0), ('qu', 0), ('qc', 0, 1, 1)]
+PLACE = {(0, 0): [('qk', 0, 0, 1)], (3, 2): [('sp', 0, 1), ('gk', 1, 1, 0)], (4, 0): [('qk', 1, 1, 0)], (10, 2): [('fg', 1, 1, 0)], (12, 0): [('sp', 1, 0)], (1, 3): [('r', 0, 1, 2), ('fg', 1, 1, 1), ('r', 1, 1, 2)], (4, 1): [('r', 1, 1, 1)], (4, 4): [('gk', 1, 1, 1)], (11, 5): [('qc', 1, 1, 0)], (4, 2): [('gk', 1, 0, 1)], (3, 0): [('r', 0, 0, 1)], (7, 4): [('r', 1, 1, 0)], (6, 0): [('gk', 1, 0, 0)], (1, 6): [('fg', 1, 0, 0), ('r', 0, 1, 1)], (6, 2): [('qk', 1, 0, 0)], (2, 4): [('r', 0, 0, 0)], (11, 1): [('r', 1, 0, 1), ('r', 1, 0, 2)], (1, 4): [('r', 0, 1, 3), ('qc', 0, 0, 1), ('fg', 1, 0, 1)], (8, 3): [('qc', 1, 0, 0)], (5, 2): [('qk', 1, 0, 1), ('qk', 1, 1, 1)], (8, 2): [('r', 1, 1, 3)], (10, 1): [('r', 1, 0, 0)], (12, 1): [('qc', 1, 0, 1)], (2, 3): [('r', 0, 0, 2)], (3, 5): [('r', 0, 0, 3)], (11, 0): [('qc', 1, 1, 1)], (3, 6): [('sp', 0, 0)], (9, 1): [('sp', 1, 1)], (0, 1): [('r', 0, 1, 0)], (11, 6): [('r', 1, 0, 3)]}
+FILL_ENGINE = {('gk', 0, 0, 1): 'S', ('gk', 1, 0, 0): 'G', ('gk', 1, 1, 0): 'V', ('gk', 1, 0, 1): 'S', ('sp', 1, 0): 'S', ('sp', 1, 1): 'S', ('sp', 0, 1): 'S', ('gk', 0, 0, 0): 'G', ('gk', 1, 1, 1): 'G', ('sp', 0, 0): 'S', ('gk', 0, 1, 0): 'G', ('gk', 0, 1, 1): 'S'}
+FLIP_ENGINES = {('fg', 0, 1, 1): 'VS'}
+COPY_ENGINE = {}
+SORTED = {('X', 1, 3): 'S', ('X', 0, 1): 'V', ('X', 1, 1): 'V', ('A', 1, 0): 'S', ('X', 0, 2): 'S', ('A', 1, 1): 'S', ('fg', 1, 0, 0): 'V', ('X', 1, 0): 'V', ('X', 1, 2): 'V'}
 PAIR = False
 FINE = 4
 HALF_FIRST = 2
@@ -191,12 +191,24 @@ def tile_lvc_pb_v_kernel(tc, assign, xp, codebook, grad_out, out_0, out_1):
 
         def group_grad_k(b, g, half, engine):
             stage = stream.tile([P, HALF, PACK], BF16, name="grad_k_grouped", align_bytes=64)
+            grad_stage["k", b, g, half] = stage
+            if engine == "G":
+                for q in range(4):
+                    cols = slice(q * P, (q + 1) * P)
+                    nc.gpsimd.tensor_scalar(
+                        out=stage[:, cols, :],
+                        in0=grad_half(b, g, half)[:, :, cols].rearrange("p t c -> p c t"),
+                        scalar1=1.0,
+                        scalar2=0.0,
+                        op0=MULT,
+                        op1=mybir.AluOpType.add,
+                    )
+                return
             copy = nc.scalar.copy if engine == "S" else nc.vector.tensor_copy
             copy(
                 out=stage[:].rearrange("p (c i) t -> p c t i", i=4),
                 in_=grad_half(b, g, half).rearrange("p t (c i) -> p c t i", i=4),
             )
-            grad_stage["k", b, g, half] = stage
 
         def quantize_grad_k(b, g, half):
             cols = slice(half * HALF, (half + 1) * HALF)

@@ -17,328 +17,328 @@ FLOPS = 2 * 2 * IMAGES * PIXELS * CHANNELS * CODEWORDS
 
 P = 128
 PACK = 4
-K_PASS = P * PACK
+PASS_K = P * PACK
 PASSES = 2
+WORDS = PASS_K // 2
 HALF = 512
-ROWS = 2
-UNIT = P * ROWS
-ORDER = [('A', 0, 0), ('A', 0, 1), ('A', 0, 2), ('A', 0, 3), ('X', 0, 0), ('X', 0, 3), ('X', 0, 1), ('A', 1, 3), ('X', 0, 2), ('A', 1, 1), ('A', 1, 2), ('A', 1, 0), ('X', 1, 1), ('X', 1, 0), ('X', 1, 2), ('X', 1, 3)]
-LOADS = [('gh', 0, 0, 0), ('gh', 0, 1, 1), ('gh', 0, 1, 0), ('u', ('A', 0, 0), 0), ('gh', 0, 0, 1), ('u', ('A', 0, 0), 1), ('u', ('A', 0, 2)), ('b', 1), ('g', 1, 1), ('g', 1, 0), ('b', 0)]
-LATER = [(0, ('u', ('X', 0, 0))), (0, ('u', ('X', 0, 2))), (0, ('u', ('A', 1, 2))), (0, ('u', ('X', 1, 0))), (3, ('u', ('A', 1, 0))), (6, ('u', ('X', 1, 2)))]
-HEAD = [('gk', 0, 0, 0), ('fg', 0, 0, 0), ('gk', 0, 1, 1), ('fg', 0, 1, 0), ('qk', 0, 0, 0), ('fg', 0, 1, 1), ('flip', 0), ('gk', 0, 1, 0), ('qk', 0, 1, 1), ('flip', 1), ('qc', 0, 0, 0), ('gk', 0, 0, 1), ('qk', 0, 1, 0), ('fg', 0, 0, 1), ('qc', 0, 1, 0), ('qu', 0), ('qc', 0, 1, 1)]
-PLACE = {(0, 0): [('qk', 0, 0, 1)], (3, 2): [('sp', 0, 1), ('gk', 1, 1, 0)], (4, 0): [('qk', 1, 1, 0)], (10, 2): [('fg', 1, 1, 0)], (12, 0): [('sp', 1, 0)], (1, 3): [('r', 0, 1, 2), ('fg', 1, 1, 1), ('r', 1, 1, 2)], (4, 1): [('r', 1, 1, 1)], (4, 4): [('gk', 1, 1, 1)], (11, 5): [('qc', 1, 1, 0)], (4, 2): [('gk', 1, 0, 1)], (3, 0): [('r', 0, 0, 1)], (7, 4): [('r', 1, 1, 0)], (6, 0): [('gk', 1, 0, 0)], (1, 6): [('fg', 1, 0, 0), ('r', 0, 1, 1)], (6, 2): [('qk', 1, 0, 0)], (2, 4): [('r', 0, 0, 0)], (11, 1): [('r', 1, 0, 1), ('r', 1, 0, 2)], (1, 4): [('r', 0, 1, 3), ('qc', 0, 0, 1), ('fg', 1, 0, 1)], (8, 3): [('qc', 1, 0, 0)], (5, 2): [('qk', 1, 0, 1), ('qk', 1, 1, 1)], (8, 2): [('r', 1, 1, 3)], (10, 1): [('r', 1, 0, 0)], (12, 1): [('qc', 1, 0, 1)], (2, 3): [('r', 0, 0, 2)], (3, 5): [('r', 0, 0, 3)], (11, 0): [('qc', 1, 1, 1)], (3, 6): [('sp', 0, 0)], (9, 1): [('sp', 1, 1)], (0, 1): [('r', 0, 1, 0)], (11, 6): [('r', 1, 0, 3)]}
-FILL_ENGINE = {('gk', 0, 0, 1): 'S', ('gk', 1, 0, 0): 'G', ('gk', 1, 1, 0): 'V', ('gk', 1, 0, 1): 'S', ('sp', 1, 0): 'S', ('sp', 1, 1): 'S', ('sp', 0, 1): 'S', ('gk', 0, 0, 0): 'G', ('gk', 1, 1, 1): 'G', ('sp', 0, 0): 'S', ('gk', 0, 1, 0): 'G', ('gk', 0, 1, 1): 'S'}
-FLIP_ENGINES = {('fg', 0, 1, 1): 'VS'}
-COPY_ENGINE = {}
-SORTED = {('X', 1, 3): 'S', ('X', 0, 1): 'V', ('X', 1, 1): 'V', ('A', 1, 0): 'S', ('X', 0, 2): 'S', ('A', 1, 1): 'S', ('fg', 1, 0, 0): 'V', ('X', 1, 0): 'V', ('X', 1, 2): 'V'}
-PAIR = False
-FINE = 4
-HALF_FIRST = 2
-UNIT_BUFS = 3
-ROW_BUFS = 5
-RESULT_BUFS = 4
-FLIP_BANKS = 4
-SUM_BANKS = 4
+UNIT_ROWS = 2
+LOAD_ROWS = 4
+
+FINE_STORES = 4
+LOAD_AHEAD = 6
+
+STEPS = (
+    ((0, 0), (("dot", 0, 0, 3), ("dot", 0, 0, 0)), ()),
+    ((0, 0), (("dot", 0, 0, 2), ("dot", 0, 0, 1), ("transpose", 1, 0, 0)), ()),
+    (
+        (0, 0),
+        (("spread", 0, 0), ("transpose", 1, 1, 0), ("transpose", 1, 1, 1), ("interleave", 1, 0, 1, "vector")),
+        (("dot", 1, 0, 3), ("dot", 0, 1, 1), ("quantize_c", 0, 1, 0)),
+    ),
+    (
+        (0, 0),
+        (
+            ("dot", 0, 1, 0),
+            ("dot", 0, 1, 2),
+            ("quantize_k", 1, 0, 1),
+            ("dot", 0, 1, 3),
+            ("interleave", 1, 1, 0, "scalar"),
+        ),
+        (),
+    ),
+    ((1, 0), (("spread", 0, 1), ("dot", 1, 1, 3)), ()),
+    (
+        (1, 0),
+        (("interleave", 1, 1, 1, "scalar"), ("dot", 1, 0, 0)),
+        (("quantize_k", 1, 1, 0), ("interleave", 1, 0, 0, "scalar")),
+    ),
+    ((1, 0), (("transpose", 1, 0, 1),), (("quantize_k", 1, 0, 0), ("quantize_k", 1, 1, 1))),
+    ((0, 1), (), ()),
+    ((1, 0), (("dot", 1, 1, 0),), (("dot", 1, 0, 1),)),
+    ((0, 1), (("dot", 1, 0, 2),), ()),
+    ((0, 1), (("dot", 1, 1, 2), ("dot", 1, 1, 1), ("quantize_c", 1, 1, 0)), ()),
+    (
+        (1, 1),
+        (("quantize_c", 1, 0, 0), ("spread", 1, 0), ("quantize_c", 1, 0, 1), ("spread", 1, 1), ("quantize_c", 1, 1, 1)),
+        (),
+    ),
+    ((1, 1), (), ()),
+    ((1, 1), (), ()),
+    ((0, 1), (), ()),
+    ((1, 1), (), ()),
+)
+
+VECTOR_SHARES_TRANSPOSES = (1, 3)
+VECTOR_SHARES_RESULTS = (3,)
+SORTED_FIRST = (11, 14, 15)
 
 
 def tile_lvc_pb_v_kernel(tc, assign, xp, codebook, grad_out, out_0, out_1):
     nc = tc.nc
+
+    units = []
+    for step in STEPS:
+        units.append(step[0] + (len([u for u in units if u[:2] == step[0]]),))
+
+    def copy_on(engine):
+        return nc.scalar.copy if engine == "scalar" else nc.vector.tensor_copy
+
     with ExitStack() as ctx:
         keep = ctx.enter_context(tc.tile_pool(name="keep", bufs=1))
         stream = ctx.enter_context(tc.tile_pool(name="stream", bufs=3))
-        flips = ctx.enter_context(tc.psum_pool(name="flips", bufs=FLIP_BANKS))
-        sums = ctx.enter_context(tc.psum_pool(name="sums", bufs=SUM_BANKS))
+        flips = ctx.enter_context(tc.psum_pool(name="flips", bufs=4))
+        sums = ctx.enter_context(tc.psum_pool(name="sums", bufs=4))
 
-        ident = keep.tile([P, P], F32, name="ident")
-        make_identity(nc, ident[:])
+        identity = keep.tile([P, P], F32, name="identity")
+        make_identity(nc, identity[:])
 
-        grad = {}
-        grad_k_codes, grad_k_scales = {}, {}
-        grad_c_codes, grad_c_scales = {}, {}
+        grad, book = {}, {}
+        k_codes, k_scales, c_codes, c_scales = {}, {}, {}, {}
         r_column, r_rows = {}, {}
+        for g in range(PASSES):
+            book[g] = keep.tile([P, PACK, CHANNELS], BF16, name="book_%d" % g)
         for b in range(IMAGES):
             for g in range(PASSES):
-                shape = [P, 2, PACK, HALF] if b == 0 else [P, PACK, CHANNELS]
-                grad[b, g] = keep.tile(shape, BF16, name="grad_%d_%d" % (b, g), align_bytes=64)
-            grad_k_codes[b] = keep.tile([P, PASSES, CHANNELS], U32, name="grad_k_codes_%d" % b, align_bytes=64)
-            grad_k_scales[b] = keep.tile([P, PASSES, CHANNELS], U8, name="grad_k_scales_%d" % b, align_bytes=64)
-            grad_c_codes[b] = keep.tile([P, PASSES, CODEWORDS], U32, name="grad_c_codes_%d" % b, align_bytes=64)
-            grad_c_scales[b] = keep.tile([P, PASSES, CODEWORDS], U8, name="grad_c_scales_%d" % b, align_bytes=64)
+                grad[b, g] = keep.tile([P, PACK, CHANNELS], BF16, name="grad_%d_%d" % (b, g))
+            k_codes[b] = keep.tile([P, PASSES, CHANNELS], U32, name="k_codes_%d" % b, align_bytes=64)
+            k_scales[b] = keep.tile([P, PASSES, CHANNELS], U8, name="k_scales_%d" % b, align_bytes=64)
+            c_codes[b] = keep.tile([P, PASSES, CODEWORDS], U32, name="c_codes_%d" % b, align_bytes=64)
+            c_scales[b] = keep.tile([P, PASSES, CODEWORDS], U8, name="c_scales_%d" % b, align_bytes=64)
             r_column[b] = keep.tile([P, PASSES * PACK], F32, name="r_column_%d" % b)
             r_rows[b] = keep.tile([P, CODEWORDS], F32, name="r_rows_%d" % b)
-        words = {}
-        for g in range(PASSES):
-            words[g] = keep.tile([P, PACK, CHANNELS], BF16, name="book_%d" % g, align_bytes=64)
-        book = words
+
+        def columns_of(half):
+            return slice(half * HALF, (half + 1) * HALF)
 
         def codeword_rows(matrix, g):
-            return matrix[g * K_PASS : (g + 1) * K_PASS, :].rearrange("(p j) c -> p j c", j=PACK)
+            return matrix[g * PASS_K : (g + 1) * PASS_K, :].rearrange("(p j) c -> p j c", j=PACK)
 
-        def load_grad_half(b, g, half):
-            cols = slice(half * HALF, (half + 1) * HALF)
-            nc.sync.dma_start(out=grad[b, g][:, half], in_=codeword_rows(grad_out[b], g)[:, :, cols])
-
-        def grad_half(b, g, half):
-            if b == 0:
-                return grad[b, g][:, half]
-            return grad[b, g][:, :, half * HALF : (half + 1) * HALF]
-
-        def load_grad(b, g):
-            nc.sync.dma_start(out=grad[b, g][:], in_=codeword_rows(grad_out[b], g))
+        def load_grad(b, g, rows=slice(0, PACK)):
+            nc.sync.dma_start(out=grad[b, g][:, rows, :], in_=codeword_rows(grad_out[b], g)[:, rows, :])
 
         def load_book(g):
             nc.sync.dma_start(out=book[g][:], in_=codeword_rows(codebook, g))
 
-        raw = {}
+        def pixel_rows(tensor, unit):
+            start = unit[2] // 2 * P * LOAD_ROWS
+            return tensor[unit[1], start : start + P * LOAD_ROWS, :].rearrange("(p j) w -> p j w", j=LOAD_ROWS)
 
-        def load_rows(u, part=None):
-            kind, b, i = u
-            source = (assign if kind == "A" else xp)[b, (i // 2) * 2 * UNIT : (i // 2 + 1) * 2 * UNIT, :].rearrange(
-                "(p j) k -> p j k", j=2 * ROWS
-            )
-            key = (kind, b, i // 2)
-            if key not in raw:
-                rows = stream.tile([P, 2 * ROWS, 1024], BF16, name="rows", bufs=ROW_BUFS, align_bytes=64)
-                raw[key] = rows
-            span = slice(0, 2 * ROWS) if part is None else slice(part * ROWS, (part + 1) * ROWS)
-            nc.sync.dma_start(out=raw[key][:, span, :], in_=source[:, span, :])
+        def pair_of(unit):
+            return (unit[0], unit[1], unit[2] // 2)
 
-        def sort_words(words, engine):
-            ordered = stream.tile([P, 2, 2, 2, P], F32, name="ordered", bufs=2)
-            copy = nc.scalar.copy if engine == "S" else nc.vector.tensor_copy
-            return ordered, copy
+        def rows_of(unit):
+            return slice(unit[2] % 2 * UNIT_ROWS, (unit[2] % 2 + 1) * UNIT_ROWS)
+
+        pixels = {}
+
+        def load_pixels(unit, rows=slice(0, LOAD_ROWS)):
+            if pair_of(unit) not in pixels:
+                loaded = stream.tile([P, LOAD_ROWS, 1024], BF16, name="loaded", bufs=5)
+                pixels[pair_of(unit)] = loaded
+            source = pixel_rows((assign, xp)[unit[0]], unit)
+            nc.sync.dma_start(out=pixels[pair_of(unit)][:, rows, :], in_=source[:, rows, :])
 
         grouped = {}
 
-        def flip_unit(u):
-            engines = FLIP_ENGINES.get(u, "SS")
-            kind, b, i = u
-            wide = raw[kind, b, i // 2][:].bitcast(F32)[:, (i % 2) * ROWS : (i % 2 + 1) * ROWS, :]
-            engine = SORTED.get(u)
-            if engine:
-                ordered, copy = sort_words(None, engine)
-                copy(out=ordered[:].rearrange("p j h w n -> p (j h) w n"), in_=wide.rearrange("p j (h n w) -> p (j h) w n", h=PASSES, w=2))
-            stage = stream.tile([P, ROWS, PASSES, P, PACK], BF16, name="unit_grouped", bufs=UNIT_BUFS, align_bytes=64)
-            for j in range(ROWS):
-                bank = flips.tile([P, PASSES, 2, P], F32, name="flip_bank")
+        def transpose_unit(step):
+            unit = units[step]
+            words = pixels[pair_of(unit)][:].bitcast(F32)[:, rows_of(unit), :]
+            if step in SORTED_FIRST:
+                ordered = stream.tile([P, UNIT_ROWS, PASSES, 2, P], F32, name="ordered", bufs=2)
+                nc.scalar.copy(
+                    out=ordered[:].rearrange("p j h w q -> p (j h) w q"),
+                    in_=words.rearrange("p j (h q w) -> p (j h) w q", h=PASSES, w=2),
+                )
+            target = stream.tile([P, UNIT_ROWS, PASSES, P, PACK], BF16, name="unit_grouped", align_bytes=64)
+            for j in range(UNIT_ROWS):
+                bank = flips.tile([P, PASSES, 2, P], F32, name="bank")
                 for h in range(PASSES):
                     for w in range(2):
-                        columns = ordered[:, j, h, w, :] if engine else wide[:, j, 256 * h + w : 256 * (h + 1) : 2]
-                        nc.tensor.transpose(bank[:, h, w, :], columns, ident[:])
-                copy = nc.scalar.copy if engines[j] == "S" else nc.vector.tensor_copy
-                copy(out=stage[:, j].bitcast(F32), in_=bank[:].rearrange("p h w n -> p h n w"))
-            grouped[u] = stage
+                        if step in SORTED_FIRST:
+                            source = ordered[:, j, h, w, :]
+                        else:
+                            source = words[:, j, WORDS * h + w : WORDS * (h + 1) : 2]
+                        nc.tensor.transpose(bank[:, h, w, :], source, identity[:])
+                copy = copy_on("vector" if step in VECTOR_SHARES_TRANSPOSES and j == 0 else "scalar")
+                copy(out=target[:, j].bitcast(F32), in_=bank[:].rearrange("p h w n -> p h n w"))
+            grouped[unit] = target
 
-        coded = {}
+        codes_of = {}
 
-        def quantize_unit(u):
-            stage = grouped.pop(u)
-            codes = stream.tile([P, ROWS * PASSES * P], U32, name="unit_codes", align_bytes=64)
-            scales = stream.tile([P, ROWS * PASSES * P], U8, name="unit_scales", align_bytes=64)
+        def quantize_unit(unit):
+            codes = stream.tile([P, UNIT_ROWS * PASSES * P], U32, name="unit_codes", align_bytes=64)
+            scales = stream.tile([P, UNIT_ROWS * PASSES * P], U8, name="unit_scales", align_bytes=64)
             nc.vector.quantize_mx(
-                out=codes[:].bitcast(E4M3X4), scales=scales[:], in_=stage[:].rearrange("p j h n t -> p (j h n t)")
+                out=codes[:].bitcast(E4M3X4),
+                scales=scales[:],
+                in_=grouped.pop(unit)[:].rearrange("p j h n t -> p (j h n t)"),
             )
-            coded[u] = (codes, scales)
+            codes_of[unit] = (codes, scales)
 
-        result = {}
-
-        def multiply(u, j, half):
-            kind, b, i = u
-            codes, scales = coded[u]
-            moving, moving_scales = (
-                (grad_k_codes[b], grad_k_scales[b]) if kind == "A" else (grad_c_codes[b], grad_c_scales[b])
+        def interleave(b, g, half, engine):
+            target = stream.tile([P, HALF, PACK], BF16, name="k_grouped", align_bytes=64)
+            copy_on(engine)(
+                out=target[:].rearrange("p (c i) j -> p c j i", i=4),
+                in_=grad[b, g][:, :, columns_of(half)].rearrange("p j (c i) -> p c j i", i=4),
             )
-            acc = sums.tile([P, HALF], F32, name="acc")
-            cols = slice(half * HALF, (half + 1) * HALF)
+            grouped["k", b, g, half] = target
+
+        def quantize_k(b, g, half):
+            nc.vector.quantize_mx(
+                out=k_codes[b][:, g, columns_of(half)].bitcast(E5M2X4),
+                scales=k_scales[b][:, g, columns_of(half)],
+                in_=grouped.pop(("k", b, g, half))[:].rearrange("p c j -> p (c j)"),
+            )
+
+        def transpose_grad(b, g, h):
+            words = grad[b, g][:].bitcast(F32)
+            target = stream.tile([P, PACK, P, PACK], BF16, name="c_grouped", bufs=4, align_bytes=64)
+            for first in range(0, PACK, 2):
+                bank = flips.tile([P, 2, 2, P], F32, name="bank")
+                for j in range(2):
+                    for w in range(2):
+                        source = words[:, first + j, WORDS * h + w : WORDS * (h + 1) : 2]
+                        nc.tensor.transpose(bank[:, j, w, :], source, identity[:])
+                nc.scalar.copy(
+                    out=target[:, first : first + 2].bitcast(F32), in_=bank[:].rearrange("p j w q -> p j q w")
+                )
+            grouped["c", b, g, h] = target
+
+        def quantize_c(b, g, h):
+            nc.vector.quantize_mx(
+                out=c_codes[b][:, h, columns_of(g)].bitcast(E5M2X4),
+                scales=c_scales[b][:, h, columns_of(g)],
+                in_=grouped.pop(("c", b, g, h))[:].rearrange("p j q t -> p (j q t)"),
+            )
+
+        def dot(b, g, j):
+            m = g * PACK + j
+            products = stream.tile([P, CHANNELS], F32, name="products", bufs=1)
+            nc.vector.scalar_tensor_tensor(
+                out=products[:],
+                in0=grad[b, g][:, j, :],
+                scalar=1.0,
+                in1=book[g][:, j, :],
+                op0=MULT,
+                op1=MULT,
+                accum_out=r_column[b][:, m : m + 1],
+            )
+
+        def spread(b, g):
+            bank = flips.tile([P, PACK, P], F32, name="bank")
+            for j in range(PACK):
+                m = g * PACK + j
+                nc.tensor.transpose(bank[:, j, :], r_column[b][:, m : m + 1].to_broadcast([P, P]), identity[:])
+            nc.scalar.copy(
+                out=r_rows[b][:, columns_of(g)].rearrange("n (q j) -> n q j", j=PACK),
+                in_=bank[:].rearrange("n j q -> n q j"),
+            )
+
+        jobs = {
+            "interleave": interleave,
+            "quantize_k": quantize_k,
+            "transpose": transpose_grad,
+            "quantize_c": quantize_c,
+            "dot": dot,
+            "spread": spread,
+        }
+
+        def multiply(unit, j, half):
+            codes, scales = codes_of[unit]
+            b = unit[1]
+            moving, moving_scales = ((k_codes[b], k_scales[b]), (c_codes[b], c_scales[b]))[unit[0]]
+            total = sums.tile([P, HALF], F32, name="total")
             for h in range(PASSES):
                 own = slice((j * PASSES + h) * P, (j * PASSES + h + 1) * P)
                 nc.tensor.matmul_mx(
-                    out=acc[:],
+                    out=total[:],
                     lhsT=codes[:, own].bitcast(E4M3X4),
                     lhsT_scale=scales[:, own],
-                    rhs=moving[:, h, cols].bitcast(E5M2X4),
-                    rhs_scale=moving_scales[:, h, cols],
+                    rhs=moving[:, h, columns_of(half)].bitcast(E5M2X4),
+                    rhs_scale=moving_scales[:, h, columns_of(half)],
                     start=(h == 0),
                     stop=(h == PASSES - 1),
                 )
-            if u not in result:
-                result[u] = stream.tile([P, ROWS, 1024], F32, name="result", bufs=RESULT_BUFS)
-            return acc
+            return total
 
-        def finish(u, j, half, acc, engine="S"):
-            kind, b, i = u
-            cols = slice(half * HALF, (half + 1) * HALF)
-            target = result[u][:, j, cols]
-            if kind == "A":
-                copy = nc.scalar.copy if engine == "S" else nc.vector.tensor_copy
-                copy(out=target, in_=acc[:])
+        def finish(step, result, j, half, total):
+            output, b, i = units[step]
+            target = result[:, j, columns_of(half)]
+            if output == 0:
+                copy = copy_on("vector" if step in VECTOR_SHARES_RESULTS and half == 0 else "scalar")
+                copy(out=target, in_=total[:])
             else:
                 nc.vector.tensor_tensor(
-                    out=target.rearrange("p (q j) -> p q j", j=PACK),
-                    in0=acc[:].rearrange("p (j q) -> p q j", j=PACK),
-                    in1=r_rows[b][:, cols].rearrange("p (q j) -> p q j", j=PACK),
+                    out=target.rearrange("n (q j) -> n q j", j=PACK),
+                    in0=total[:].rearrange("n (j q) -> n q j", j=PACK),
+                    in1=r_rows[b][:, columns_of(half)].rearrange("n (q j) -> n q j", j=PACK),
                     op=SUBTRACT,
                 )
 
-        def store(u, rows=slice(0, ROWS), cols=slice(0, 1024)):
-            kind, b, i = u
-            target = (out_0 if kind == "A" else out_1)[b, (i // 2) * 2 * UNIT : (i // 2 + 1) * 2 * UNIT, :].rearrange(
-                "(p j) c -> p j c", j=2 * ROWS
-            )[:, (i % 2) * ROWS : (i % 2 + 1) * ROWS, :]
-            nc.sync.dma_start(out=target[:, rows, cols], in_=result[u][:, rows, cols])
-
-        grad_stage = {}
-
-        def group_grad_k(b, g, half, engine):
-            stage = stream.tile([P, HALF, PACK], BF16, name="grad_k_grouped", align_bytes=64)
-            grad_stage["k", b, g, half] = stage
-            if engine == "G":
-                for q in range(4):
-                    cols = slice(q * P, (q + 1) * P)
-                    nc.gpsimd.tensor_scalar(
-                        out=stage[:, cols, :],
-                        in0=grad_half(b, g, half)[:, :, cols].rearrange("p t c -> p c t"),
-                        scalar1=1.0,
-                        scalar2=0.0,
-                        op0=MULT,
-                        op1=mybir.AluOpType.add,
-                    )
-                return
-            copy = nc.scalar.copy if engine == "S" else nc.vector.tensor_copy
-            copy(
-                out=stage[:].rearrange("p (c i) t -> p c t i", i=4),
-                in_=grad_half(b, g, half).rearrange("p t (c i) -> p c t i", i=4),
-            )
-
-        def quantize_grad_k(b, g, half):
-            cols = slice(half * HALF, (half + 1) * HALF)
-            nc.vector.quantize_mx(
-                out=grad_k_codes[b][:, g, cols].bitcast(E5M2X4),
-                scales=grad_k_scales[b][:, g, cols],
-                in_=grad_stage.pop(("k", b, g, half))[:].rearrange("p c t -> p (c t)"),
-            )
-
-        def flip_grad(b, g, h):
-            engines = FLIP_ENGINES.get(("fg", b, g, h), "SS")
-            wide = grad_half(b, g, h).bitcast(F32)
-            engine = SORTED.get(("fg", b, g, h))
-            if engine:
-                ordered, copy = sort_words(None, engine)
-                copy(out=ordered[:].rearrange("p j h w n -> p (j h) w n"), in_=wide.rearrange("p j (n w) -> p j w n", w=2))
-            stage = stream.tile([P, PACK, P, PACK], BF16, name="grad_c_grouped", bufs=4, align_bytes=64)
-            for pair in range(2):
-                bank = flips.tile([P, 2, 2, P], F32, name="flip_bank")
-                for jj in range(2):
-                    for w in range(2):
-                        columns = ordered[:, pair, jj, w, :] if engine else wide[:, 2 * pair + jj, w::2]
-                        nc.tensor.transpose(bank[:, jj, w, :], columns, ident[:])
-                copy = nc.scalar.copy if engines[pair] == "S" else nc.vector.tensor_copy
-                copy(
-                    out=stage[:, 2 * pair : 2 * pair + 2].bitcast(F32), in_=bank[:].rearrange("p j w n -> p j n w")
-                )
-            grad_stage["c", b, g, h] = stage
-
-        def quantize_grad_c(b, g, h):
-            cols = slice(g * K_PASS, (g + 1) * K_PASS)
-            nc.vector.quantize_mx(
-                out=grad_c_codes[b][:, h, cols].bitcast(E5M2X4),
-                scales=grad_c_scales[b][:, h, cols],
-                in_=grad_stage.pop(("c", b, g, h))[:].rearrange("p j n t -> p (j n t)"),
-            )
-
-        def sum_r(b, g, j):
-            product = stream.tile([P, 2, HALF], F32, name="product", bufs=1)
-            row = grad[b, g][:, :, j, :] if b == 0 else grad[b, g][:, j, :].rearrange("p (h c) -> p h c", h=2)
-            nc.vector.scalar_tensor_tensor(
-                out=product[:],
-                in0=row,
-                scalar=1.0,
-                in1=book[g][:, j, :].rearrange("p (h c) -> p h c", h=2),
-                op0=MULT,
-                op1=MULT,
-                accum_out=r_column[b][:, g * PACK + j : g * PACK + j + 1],
-            )
-
-        def spread_r(b, g, engine):
-            bank = flips.tile([P, PACK, P], F32, name="flip_bank")
-            for j in range(PACK):
-                m = g * PACK + j
-                nc.tensor.transpose(bank[:, j, :], r_column[b][:, m : m + 1].to_broadcast([P, P]), ident[:])
-            copy = nc.scalar.copy if engine == "S" else nc.vector.tensor_copy
-            copy(
-                out=r_rows[b][:, g * K_PASS : (g + 1) * K_PASS].rearrange("p (q j) -> p q j", j=PACK),
-                in_=bank[:].rearrange("p j q -> p q j"),
-            )
-
-        def fill(f):
-            kind, b, g, *rest = f
-            engine = FILL_ENGINE.get(f, "S" if kind == "sp" else "V")
-            if kind == "gk":
-                group_grad_k(b, g, rest[0], engine)
-            elif kind == "qk":
-                quantize_grad_k(b, g, rest[0])
-            elif kind == "fg":
-                flip_grad(b, g, rest[0])
-            elif kind == "qc":
-                quantize_grad_c(b, g, rest[0])
-            elif kind == "r":
-                sum_r(b, g, rest[0])
-            else:
-                spread_r(b, g, engine)
-
-        def load(x):
-            if x[0] == "gh":
-                load_grad_half(*x[1:])
-            elif x[0] == "g":
-                load_grad(*x[1:])
-            elif x[0] == "b":
-                load_book(x[1])
-            else:
-                load_rows(*x[1:])
+        def store(unit, result, rows=slice(0, UNIT_ROWS), columns=slice(0, 1024)):
+            target = pixel_rows((out_0, out_1)[unit[0]], unit)[:, rows_of(unit), :]
+            nc.sync.dma_start(out=target[:, rows, columns], in_=result[:, rows, columns])
 
         with tc.manual_schedule():
-            done = set()
-            for x in LOADS:
-                load(x)
-            for f in HEAD:
-                if f[0] == "flip":
-                    flip_unit(ORDER[f[1]])
-                    done.add(f[1])
-                elif f[0] == "qu":
-                    quantize_unit(ORDER[f[1]])
-                    done.add(("q", f[1]))
-                else:
-                    fill(f)
-            later = list(LATER)
-            n = len(ORDER)
-            for s, u in enumerate(ORDER):
-                for f in PLACE.get((s, 0), []):
-                    fill(f)
-                ahead = ([s + 2, s + 3] if s % 2 == 0 else []) if PAIR else [s + 2]
-                for d in ahead:
-                    if d < n and d not in done:
-                        done.add(d)
-                        flip_unit(ORDER[d])
-                for f in PLACE.get((s, 1), []):
-                    fill(f)
-                if s + 1 < n and ("q", s + 1) not in done:
-                    quantize_unit(ORDER[s + 1])
-                for f in PLACE.get((s, 2), []):
-                    fill(f)
-                last = s == n - 1
-                if s < HALF_FIRST:
-                    groups = [(half, j) for half in range(2) for j in range(ROWS)]
-                else:
-                    groups = [(half, j) for j in range(ROWS) for half in range(2)]
-                for k, (half, j) in enumerate(groups):
-                    finish(u, j, half, multiply(u, j, half), COPY_ENGINE.get((u, k), "S"))
-                    for f in PLACE.get((s, 3 + k), []):
-                        fill(f)
-                    if last:
-                        store(u, slice(j, j + 1), slice(half * HALF, (half + 1) * HALF))
-                    elif s >= n - FINE and half == 1:
-                        store(u, slice(j, j + 1))
-                while later and later[0][0] <= s:
-                    load(later.pop(0)[1])
-                if s < n - FINE:
-                    store(u)
+            first_rows, last_rows = slice(0, 2), slice(2, 4)
+            load_grad(0, 0, first_rows)
+            load_grad(0, 0, last_rows)
+            load_pixels(units[0], rows_of(units[0]))
+            load_grad(0, 1, first_rows)
+            load_grad(0, 1, last_rows)
+            load_pixels(units[1], rows_of(units[1]))
+            load_pixels(units[2])
+            load_book(0)
+            load_grad(1, 0)
+            load_book(1)
+            load_grad(1, 1)
+            loads_due = {}
+            asked = [pair_of(units[0]), pair_of(units[2])]
+            for step, unit in enumerate(units):
+                if pair_of(unit) not in asked:
+                    asked.append(pair_of(unit))
+                    loads_due.setdefault(max(0, step - LOAD_AHEAD), []).append(unit)
+
+            interleave(0, 0, 0, "vector")
+            transpose_grad(0, 0, 0)
+            interleave(0, 0, 1, "vector")
+            quantize_c(0, 0, 0)
+            quantize_k(0, 0, 0)
+            interleave(0, 1, 0, "vector")
+            transpose_grad(0, 0, 1)
+            quantize_c(0, 0, 1)
+            transpose_unit(0)
+            transpose_grad(0, 1, 1)
+            quantize_c(0, 1, 1)
+            transpose_grad(0, 1, 0)
+            quantize_unit(units[0])
+            quantize_k(0, 0, 1)
+            quantize_k(0, 1, 0)
+            interleave(0, 1, 1, "scalar")
+            transpose_unit(1)
+            quantize_k(0, 1, 1)
+
+            for step, unit in enumerate(units):
+                before, between = STEPS[step][1:]
+                for job in before:
+                    jobs[job[0]](*job[1:])
+                if step + 2 < len(units):
+                    transpose_unit(step + 2)
+                if step + 1 < len(units):
+                    quantize_unit(units[step + 1])
+                for job in between:
+                    jobs[job[0]](*job[1:])
+                result = stream.tile([P, UNIT_ROWS, 1024], F32, name="result", bufs=4)
+                is_last = step == len(units) - 1
+                is_fine = step >= len(units) - FINE_STORES
+                for j in range(UNIT_ROWS):
+                    for half in range(2):
+                        finish(step, result, j, half, multiply(unit, j, half))
+                        if is_last:
+                            store(unit, result, slice(j, j + 1), columns_of(half))
+                    if is_fine and not is_last:
+                        store(unit, result, slice(j, j + 1))
+                for due in loads_due.get(step, []):
+                    load_pixels(due)
+                if not is_fine:
+                    store(unit, result)

from contextlib import ExitStack

import concourse.mybir as mybir
from concourse.masks import make_identity

F32 = mybir.dt.float32
BF16 = mybir.dt.bfloat16
U32 = mybir.dt.uint32
U8 = mybir.dt.uint8
E4M3X4 = mybir.dt.float8_e4m3fn_x4
E5M2X4 = mybir.dt.float8_e5m2_x4
MULT = mybir.AluOpType.mult
SUBTRACT = mybir.AluOpType.subtract

IMAGES, PIXELS, CHANNELS, CODEWORDS = 2, 1024, 1024, 1024
FLOPS = 2 * 2 * IMAGES * PIXELS * CHANNELS * CODEWORDS

P = 128
PACK = 4
PASS_K = P * PACK
PASSES = 2
WORDS = PASS_K // 2
HALF = 512
UNIT_ROWS = 2
LOAD_ROWS = 4

FINE_STORES = 4
LOAD_AHEAD = 6

STEPS = (
    ((0, 0), (("dot", 0, 0, 3), ("dot", 0, 0, 0)), ()),
    ((0, 0), (("dot", 0, 0, 2), ("dot", 0, 0, 1), ("transpose", 1, 0, 0)), ()),
    (
        (0, 0),
        (("spread", 0, 0), ("transpose", 1, 1, 0), ("transpose", 1, 1, 1), ("interleave", 1, 0, 1, "vector")),
        (("dot", 1, 0, 3), ("dot", 0, 1, 1), ("quantize_c", 0, 1, 0)),
    ),
    (
        (0, 0),
        (
            ("dot", 0, 1, 0),
            ("dot", 0, 1, 2),
            ("quantize_k", 1, 0, 1),
            ("dot", 0, 1, 3),
            ("interleave", 1, 1, 0, "scalar"),
        ),
        (),
    ),
    ((1, 0), (("spread", 0, 1), ("dot", 1, 1, 3)), ()),
    (
        (1, 0),
        (("interleave", 1, 1, 1, "scalar"), ("dot", 1, 0, 0)),
        (("quantize_k", 1, 1, 0), ("interleave", 1, 0, 0, "scalar")),
    ),
    ((1, 0), (("transpose", 1, 0, 1),), (("quantize_k", 1, 0, 0), ("quantize_k", 1, 1, 1))),
    ((0, 1), (), ()),
    ((1, 0), (("dot", 1, 1, 0),), (("dot", 1, 0, 1),)),
    ((0, 1), (("dot", 1, 0, 2),), ()),
    ((0, 1), (("dot", 1, 1, 2), ("dot", 1, 1, 1), ("quantize_c", 1, 1, 0)), ()),
    (
        (1, 1),
        (("quantize_c", 1, 0, 0), ("spread", 1, 0), ("quantize_c", 1, 0, 1), ("spread", 1, 1), ("quantize_c", 1, 1, 1)),
        (),
    ),
    ((1, 1), (), ()),
    ((1, 1), (), ()),
    ((0, 1), (), ()),
    ((1, 1), (), ()),
)

VECTOR_SHARES_TRANSPOSES = (1, 3)
VECTOR_SHARES_RESULTS = (3,)
SORTED_FIRST = (11, 14, 15)


def tile_lvc_pb_v_kernel(tc, assign, xp, codebook, grad_out, out_0, out_1):
    nc = tc.nc

    units = []
    for step in STEPS:
        units.append(step[0] + (len([u for u in units if u[:2] == step[0]]),))

    def copy_on(engine):
        return nc.scalar.copy if engine == "scalar" else nc.vector.tensor_copy

    with ExitStack() as ctx:
        keep = ctx.enter_context(tc.tile_pool(name="keep", bufs=1))
        stream = ctx.enter_context(tc.tile_pool(name="stream", bufs=3))
        flips = ctx.enter_context(tc.psum_pool(name="flips", bufs=4))
        sums = ctx.enter_context(tc.psum_pool(name="sums", bufs=4))

        identity = keep.tile([P, P], F32, name="identity")
        make_identity(nc, identity[:])

        grad, book = {}, {}
        k_codes, k_scales, c_codes, c_scales = {}, {}, {}, {}
        r_column, r_rows = {}, {}
        for g in range(PASSES):
            book[g] = keep.tile([P, PACK, CHANNELS], BF16, name="book_%d" % g)
        for b in range(IMAGES):
            for g in range(PASSES):
                grad[b, g] = keep.tile([P, PACK, CHANNELS], BF16, name="grad_%d_%d" % (b, g))
            k_codes[b] = keep.tile([P, PASSES, CHANNELS], U32, name="k_codes_%d" % b, align_bytes=64)
            k_scales[b] = keep.tile([P, PASSES, CHANNELS], U8, name="k_scales_%d" % b, align_bytes=64)
            c_codes[b] = keep.tile([P, PASSES, CODEWORDS], U32, name="c_codes_%d" % b, align_bytes=64)
            c_scales[b] = keep.tile([P, PASSES, CODEWORDS], U8, name="c_scales_%d" % b, align_bytes=64)
            r_column[b] = keep.tile([P, PASSES * PACK], F32, name="r_column_%d" % b)
            r_rows[b] = keep.tile([P, CODEWORDS], F32, name="r_rows_%d" % b)

        def columns_of(half):
            return slice(half * HALF, (half + 1) * HALF)

        def codeword_rows(matrix, g):
            return matrix[g * PASS_K : (g + 1) * PASS_K, :].rearrange("(p j) c -> p j c", j=PACK)

        def load_grad(b, g, rows=slice(0, PACK)):
            nc.sync.dma_start(out=grad[b, g][:, rows, :], in_=codeword_rows(grad_out[b], g)[:, rows, :])

        def load_book(g):
            nc.sync.dma_start(out=book[g][:], in_=codeword_rows(codebook, g))

        def pixel_rows(tensor, unit):
            start = unit[2] // 2 * P * LOAD_ROWS
            return tensor[unit[1], start : start + P * LOAD_ROWS, :].rearrange("(p j) w -> p j w", j=LOAD_ROWS)

        def pair_of(unit):
            return (unit[0], unit[1], unit[2] // 2)

        def rows_of(unit):
            return slice(unit[2] % 2 * UNIT_ROWS, (unit[2] % 2 + 1) * UNIT_ROWS)

        pixels = {}

        def load_pixels(unit, rows=slice(0, LOAD_ROWS)):
            if pair_of(unit) not in pixels:
                loaded = stream.tile([P, LOAD_ROWS, 1024], BF16, name="loaded", bufs=5)
                pixels[pair_of(unit)] = loaded
            source = pixel_rows((assign, xp)[unit[0]], unit)
            nc.sync.dma_start(out=pixels[pair_of(unit)][:, rows, :], in_=source[:, rows, :])

        grouped = {}

        def transpose_unit(step):
            unit = units[step]
            words = pixels[pair_of(unit)][:].bitcast(F32)[:, rows_of(unit), :]
            if step in SORTED_FIRST:
                ordered = stream.tile([P, UNIT_ROWS, PASSES, 2, P], F32, name="ordered", bufs=2)
                nc.scalar.copy(
                    out=ordered[:].rearrange("p j h w q -> p (j h) w q"),
                    in_=words.rearrange("p j (h q w) -> p (j h) w q", h=PASSES, w=2),
                )
            target = stream.tile([P, UNIT_ROWS, PASSES, P, PACK], BF16, name="unit_grouped", align_bytes=64)
            for j in range(UNIT_ROWS):
                bank = flips.tile([P, PASSES, 2, P], F32, name="bank")
                for h in range(PASSES):
                    for w in range(2):
                        if step in SORTED_FIRST:
                            source = ordered[:, j, h, w, :]
                        else:
                            source = words[:, j, WORDS * h + w : WORDS * (h + 1) : 2]
                        nc.tensor.transpose(bank[:, h, w, :], source, identity[:])
                copy = copy_on("vector" if step in VECTOR_SHARES_TRANSPOSES and j == 0 else "scalar")
                copy(out=target[:, j].bitcast(F32), in_=bank[:].rearrange("p h w n -> p h n w"))
            grouped[unit] = target

        codes_of = {}

        def quantize_unit(unit):
            codes = stream.tile([P, UNIT_ROWS * PASSES * P], U32, name="unit_codes", align_bytes=64)
            scales = stream.tile([P, UNIT_ROWS * PASSES * P], U8, name="unit_scales", align_bytes=64)
            nc.vector.quantize_mx(
                out=codes[:].bitcast(E4M3X4),
                scales=scales[:],
                in_=grouped.pop(unit)[:].rearrange("p j h n t -> p (j h n t)"),
            )
            codes_of[unit] = (codes, scales)

        def interleave(b, g, half, engine):
            target = stream.tile([P, HALF, PACK], BF16, name="k_grouped", align_bytes=64)
            copy_on(engine)(
                out=target[:].rearrange("p (c i) j -> p c j i", i=4),
                in_=grad[b, g][:, :, columns_of(half)].rearrange("p j (c i) -> p c j i", i=4),
            )
            grouped["k", b, g, half] = target

        def quantize_k(b, g, half):
            nc.vector.quantize_mx(
                out=k_codes[b][:, g, columns_of(half)].bitcast(E5M2X4),
                scales=k_scales[b][:, g, columns_of(half)],
                in_=grouped.pop(("k", b, g, half))[:].rearrange("p c j -> p (c j)"),
            )

        def transpose_grad(b, g, h):
            words = grad[b, g][:].bitcast(F32)
            target = stream.tile([P, PACK, P, PACK], BF16, name="c_grouped", bufs=4, align_bytes=64)
            for first in range(0, PACK, 2):
                bank = flips.tile([P, 2, 2, P], F32, name="bank")
                for j in range(2):
                    for w in range(2):
                        source = words[:, first + j, WORDS * h + w : WORDS * (h + 1) : 2]
                        nc.tensor.transpose(bank[:, j, w, :], source, identity[:])
                nc.scalar.copy(
                    out=target[:, first : first + 2].bitcast(F32), in_=bank[:].rearrange("p j w q -> p j q w")
                )
            grouped["c", b, g, h] = target

        def quantize_c(b, g, h):
            nc.vector.quantize_mx(
                out=c_codes[b][:, h, columns_of(g)].bitcast(E5M2X4),
                scales=c_scales[b][:, h, columns_of(g)],
                in_=grouped.pop(("c", b, g, h))[:].rearrange("p j q t -> p (j q t)"),
            )

        def dot(b, g, j):
            m = g * PACK + j
            products = stream.tile([P, CHANNELS], F32, name="products", bufs=1)
            nc.vector.scalar_tensor_tensor(
                out=products[:],
                in0=grad[b, g][:, j, :],
                scalar=1.0,
                in1=book[g][:, j, :],
                op0=MULT,
                op1=MULT,
                accum_out=r_column[b][:, m : m + 1],
            )

        def spread(b, g):
            bank = flips.tile([P, PACK, P], F32, name="bank")
            for j in range(PACK):
                m = g * PACK + j
                nc.tensor.transpose(bank[:, j, :], r_column[b][:, m : m + 1].to_broadcast([P, P]), identity[:])
            nc.scalar.copy(
                out=r_rows[b][:, columns_of(g)].rearrange("n (q j) -> n q j", j=PACK),
                in_=bank[:].rearrange("n j q -> n q j"),
            )

        jobs = {
            "interleave": interleave,
            "quantize_k": quantize_k,
            "transpose": transpose_grad,
            "quantize_c": quantize_c,
            "dot": dot,
            "spread": spread,
        }

        def multiply(unit, j, half):
            codes, scales = codes_of[unit]
            b = unit[1]
            moving, moving_scales = ((k_codes[b], k_scales[b]), (c_codes[b], c_scales[b]))[unit[0]]
            total = sums.tile([P, HALF], F32, name="total")
            for h in range(PASSES):
                own = slice((j * PASSES + h) * P, (j * PASSES + h + 1) * P)
                nc.tensor.matmul_mx(
                    out=total[:],
                    lhsT=codes[:, own].bitcast(E4M3X4),
                    lhsT_scale=scales[:, own],
                    rhs=moving[:, h, columns_of(half)].bitcast(E5M2X4),
                    rhs_scale=moving_scales[:, h, columns_of(half)],
                    start=(h == 0),
                    stop=(h == PASSES - 1),
                )
            return total

        def finish(step, result, j, half, total):
            output, b, i = units[step]
            target = result[:, j, columns_of(half)]
            if output == 0:
                copy = copy_on("vector" if step in VECTOR_SHARES_RESULTS and half == 0 else "scalar")
                copy(out=target, in_=total[:])
            else:
                nc.vector.tensor_tensor(
                    out=target.rearrange("n (q j) -> n q j", j=PACK),
                    in0=total[:].rearrange("n (j q) -> n q j", j=PACK),
                    in1=r_rows[b][:, columns_of(half)].rearrange("n (q j) -> n q j", j=PACK),
                    op=SUBTRACT,
                )

        def store(unit, result, rows=slice(0, UNIT_ROWS), columns=slice(0, 1024)):
            target = pixel_rows((out_0, out_1)[unit[0]], unit)[:, rows_of(unit), :]
            nc.sync.dma_start(out=target[:, rows, columns], in_=result[:, rows, columns])

        with tc.manual_schedule():
            first_rows, last_rows = slice(0, 2), slice(2, 4)
            load_grad(0, 0, first_rows)
            load_grad(0, 0, last_rows)
            load_pixels(units[0], rows_of(units[0]))
            load_grad(0, 1, first_rows)
            load_grad(0, 1, last_rows)
            load_pixels(units[1], rows_of(units[1]))
            load_pixels(units[2])
            load_book(0)
            load_grad(1, 0)
            load_book(1)
            load_grad(1, 1)
            loads_due = {}
            asked = [pair_of(units[0]), pair_of(units[2])]
            for step, unit in enumerate(units):
                if pair_of(unit) not in asked:
                    asked.append(pair_of(unit))
                    loads_due.setdefault(max(0, step - LOAD_AHEAD), []).append(unit)

            interleave(0, 0, 0, "vector")
            transpose_grad(0, 0, 0)
            interleave(0, 0, 1, "vector")
            quantize_c(0, 0, 0)
            quantize_k(0, 0, 0)
            interleave(0, 1, 0, "vector")
            transpose_grad(0, 0, 1)
            quantize_c(0, 0, 1)
            transpose_unit(0)
            transpose_grad(0, 1, 1)
            quantize_c(0, 1, 1)
            transpose_grad(0, 1, 0)
            quantize_unit(units[0])
            quantize_k(0, 0, 1)
            quantize_k(0, 1, 0)
            interleave(0, 1, 1, "scalar")
            transpose_unit(1)
            quantize_k(0, 1, 1)

            for step, unit in enumerate(units):
                before, between = STEPS[step][1:]
                for job in before:
                    jobs[job[0]](*job[1:])
                if step + 2 < len(units):
                    transpose_unit(step + 2)
                if step + 1 < len(units):
                    quantize_unit(units[step + 1])
                for job in between:
                    jobs[job[0]](*job[1:])
                result = stream.tile([P, UNIT_ROWS, 1024], F32, name="result", bufs=4)
                is_last = step == len(units) - 1
                is_fine = step >= len(units) - FINE_STORES
                for j in range(UNIT_ROWS):
                    for half in range(2):
                        finish(step, result, j, half, multiply(unit, j, half))
                        if is_last:
                            store(unit, result, slice(j, j + 1), columns_of(half))
                    if is_fine and not is_last:
                        store(unit, result, slice(j, j + 1))
                for due in loads_due.get(step, []):
                    load_pixels(due)
                if not is_fine:
                    store(unit, result)
